import numpy as np
import ml_dtypes


def mxq(x, axis, fmt="e4m3"):
    dtype, down = {"e4m3": (ml_dtypes.float8_e4m3fn, 7), "e5m2": (ml_dtypes.float8_e5m2, 14)}[fmt]
    v = np.moveaxis(np.asarray(x, np.float32).astype(ml_dtypes.bfloat16).astype(np.float64), axis, -1)
    blocks = v.reshape(v.shape[:-1] + (-1, 32))
    amax = np.abs(blocks).max(-1, keepdims=True)
    byte = np.maximum(np.where(amax > 0, np.frexp(amax)[1] - 1 + 127, 0) - down, 1)
    scale = np.exp2(byte - 127.0)
    codes = (blocks / scale).astype(np.float32).astype(dtype).astype(np.float64)
    return np.moveaxis((codes * scale).reshape(v.shape), -1, axis)


WIDE = False


def mx_kscale(k):
    if not WIDE:
        return np.ones(k)
    levels = np.array([10, -10, 5, -5, 0])
    a = np.random.permutation(np.resize(levels, k // 512 * 4)).reshape(k // 512, 4)
    idx = np.arange(k)
    return np.exp2(a[idx // 512, idx % 128 // 32])


BF16 = ml_dtypes.bfloat16


def bf(x):
    return np.asarray(x, np.float32).astype(BF16)


def f64(x):
    return np.asarray(x).astype(np.float64)


B, L, H, G, DEPTH = 64, 64, 512, 256, 3
EPS = 1e-5


def layernorm(v, g, b):
    mu = v.mean(-1, keepdims=True)
    var = np.square(v - mu).mean(-1, keepdims=True)
    return (v - mu) / np.sqrt(var + EPS) * g + b


def setup_inputs():
    s, t = mx_kscale(H), mx_kscale(H)
    return {"x_nodes": bf(np.random.standard_normal((B, L, H)) * s),
            "w1": bf(np.random.standard_normal((H, H)) / np.sqrt(H) / s[:, None]),
            "b1": bf(np.random.standard_normal(H) * 0.3),
            "gamma": bf((1.0 + 0.1 * np.random.standard_normal(H)) * t),
            "beta": bf(0.2 * np.random.standard_normal(H) * t),
            "w2": bf(np.random.standard_normal((H, G)) / np.sqrt(H) / t[:, None]),
            "b2": bf(np.random.standard_normal(G) * 0.3)}


def reference(x_nodes, w1, b1, gamma, beta, w2, b2):
    h = (mxq(f64(x_nodes), 2, "e4m3") @ mxq(f64(w1), 0, "e4m3")) + f64(b1)
    r = np.maximum(layernorm(h, f64(gamma), f64(beta)), 0.0)
    x1 = (mxq(r, 2, "e4m3") @ mxq(f64(w2), 0, "e4m3")) + f64(b2)
    x2 = np.broadcast_to(x1.max(axis=1, keepdims=True), x1.shape)
    return np.concatenate([x1, x2], axis=2)

@@ -1,0 +1,351 @@
+from contextlib import ExitStack
+
+import concourse.mybir as mybir
+from concourse.masks import make_identity
+
+F32 = mybir.dt.float32
+BF16 = mybir.dt.bfloat16
+U32 = mybir.dt.uint32
+U8 = mybir.dt.uint8
+FP8X4 = mybir.dt.float8_e4m3fn_x4
+ALU = mybir.AluOpType
+ACT = mybir.ActivationFunctionType
+AXIS = mybir.AxisListType
+
+P = 128
+PACK = 4
+TOKENS = 64 * 64
+NODES = 64
+H = 512
+G = 256
+EPS = 1e-5
+
+TILES = 2
+UNIT = TILES * P
+N_UNITS = TOKENS // UNIT
+UNITS_PER_GROUP = 2
+GROUP = UNITS_PER_GROUP * UNIT
+N_GROUPS = TOKENS // GROUP
+LINES_PER_UNIT = UNIT // NODES
+LINES_PER_GROUP = GROUP // NODES
+COPIES = P // LINES_PER_GROUP
+ROWS_PER_COPY = NODES // COPIES
+HALVES = G // P
+
+LAG_FIRST = 1
+LAG_NORM = 2
+LAG_FEATURES = 3
+LAG_SECOND = 5
+LAST_LAG = LAG_SECOND
+
+FLOPS = 2 * TOKENS * H * H + 2 * TOKENS * H * G
+
+
+def tile_sub_graph_pa_kernel(tc, x_nodes, w1, b1, gamma, beta, w2, b2, out):
+    nc = tc.nc
+    x_flat = x_nodes.flatten_outer_dims()
+    out_flat = out.flatten_outer_dims()
+
+    with ExitStack() as ctx:
+        ctx.enter_context(tc.manual_schedule())
+        const = ctx.enter_context(tc.tile_pool(name="const", bufs=1))
+        per_unit = ctx.enter_context(tc.tile_pool(name="per_unit", bufs=4))
+        per_tile = ctx.enter_context(tc.tile_pool(name="per_tile", bufs=4 * TILES))
+        psum_x = ctx.enter_context(tc.psum_pool(name="psum_x", bufs=1))
+        psum_h = ctx.enter_context(tc.psum_pool(name="psum_h", bufs=2))
+        psum_z = ctx.enter_context(tc.psum_pool(name="psum_z", bufs=2))
+        psum_a = ctx.enter_context(tc.psum_pool(name="psum_a", bufs=1))
+        psum_b = ctx.enter_context(tc.psum_pool(name="psum_b", bufs=1))
+        psum_s = ctx.enter_context(tc.psum_pool(name="psum_s", bufs=1))
+
+        w1_raw = const.tile([P, PACK, H], BF16)
+        nc.sync.dma_start(
+            out=w1_raw[:].rearrange("q (u e) c -> q u e c", u=2),
+            in_=w1.rearrange("(u q e) c -> q u e c", u=2, e=2),
+        )
+        x_tiles = []
+        for g in range(N_GROUPS):
+            x_sb = const.tile([P, GROUP // P, H], BF16, name="x_sb%d" % g)
+            x_tiles.append(x_sb)
+
+        def load_x(g):
+            nc.sync.dma_start(
+                out=x_tiles[g][:],
+                in_=x_flat[g * GROUP : (g + 1) * GROUP, :].rearrange("(j p) k -> p j k", p=P),
+            )
+
+        load_x(0)
+        w2_raw = const.tile([P, PACK, G], BF16)
+        nc.sync.dma_start(out=w2_raw[:], in_=w2.rearrange("(t p) n -> p t n", p=P))
+        for g in range(1, N_GROUPS):
+            load_x(g)
+
+        ident = const.tile([P, P], F32)
+        make_identity(nc, ident[:])
+        minus_half = const.tile([P, TILES], F32)
+        nc.gpsimd.memset(minus_half[:], -0.5)
+
+        bias_in = const.tile([P, H + G], BF16)
+        nc.vector.memset(bias_in[:], 0.0)
+        nc.scalar.dma_start(out=bias_in[0:1, 0:H], in_=b1.rearrange("(o k) -> o k", o=1))
+        nc.scalar.dma_start(out=bias_in[0:1, H : H + G], in_=b2.rearrange("(o k) -> o k", o=1))
+        ones = const.tile([P, P], BF16)
+        nc.vector.memset(ones[:], 1.0)
+        rows_bf = const.tile([P, P], BF16)
+        nc.vector.memset(rows_bf[:], 0.0)
+        nc.scalar.dma_start(out=rows_bf[0:4, :], in_=gamma.rearrange("(t p) -> t p", p=P))
+        nc.scalar.dma_start(out=rows_bf[4:8, :], in_=beta.rearrange("(t p) -> t p", p=P))
+        nc.scalar.dma_start(out=rows_bf[8:10, :], in_=b2.rearrange("(t p) -> t p", p=P))
+
+        rows_f32 = const.tile([P, P], F32)
+        nc.vector.tensor_copy(out=rows_f32[:], in_=rows_bf[:])
+        cols_ps = psum_s.tile([P, P], F32, tag="small")
+        nc.tensor.transpose(cols_ps[:], rows_f32[:], ident[:])
+        cols = const.tile([P, 16], F32)
+        nc.scalar.copy(out=cols[:], in_=cols_ps[:, 0:16])
+
+        b1_ps = psum_h.tile([P, H], F32, tag="h_ps")
+        nc.tensor.matmul(out=b1_ps[:], lhsT=ones[:], rhs=bias_in[:, 0:H], start=True, stop=True)
+        b1_rows = const.tile([P, H], F32)
+        nc.scalar.copy(out=b1_rows[:], in_=b1_ps[:])
+        b2_ps = psum_h.tile([P, H], F32, tag="h_ps")
+        nc.tensor.matmul(out=b2_ps[:, 0:G], lhsT=ones[:], rhs=bias_in[:, H : H + G], start=True, stop=True)
+        b2_rows = const.tile([P, G], F32)
+        nc.scalar.copy(out=b2_rows[:], in_=b2_ps[:, 0:G])
+
+        def gamma_col(t):
+            return cols[:, t : t + 1]
+
+        def beta_col(t):
+            return cols[:, 4 + t : 5 + t]
+
+        def b2_col(c):
+            return cols[:, 8 + c : 9 + c]
+
+        def quantise_weight(raw, width, label):
+            grouped = const.tile([P, width, PACK], BF16, align_bytes=64, name=label + "_grouped")
+            nc.vector.tensor_copy(out=grouped[:], in_=raw[:].rearrange("p t c -> p c t"))
+            codes = const.tile([P, width], U32, align_bytes=64, name=label + "_codes")
+            scales = const.tile([P, width], U8, align_bytes=64, name=label + "_scales")
+            nc.vector.quantize_mx(
+                out=codes[:].bitcast(FP8X4),
+                scales=scales[:],
+                in_=grouped[:].rearrange("p c t -> p (c t)"),
+            )
+            return codes, scales
+
+        w1_codes, w1_scales = quantise_weight(w1_raw, H, "w1")
+        w2_q = {}
+
+        live = {}
+
+        def x_to_partitions(unit):
+            g, part = divmod(unit, UNITS_PER_GROUP)
+            xt_ps = psum_x.tile([P, TILES, 2, P], F32)
+            for j in range(TILES):
+                words = x_tiles[g][:, part * TILES + j, :].bitcast(F32)
+                for u in range(2):
+                    nc.tensor.transpose(xt_ps[:, j, u, :], words[:, u * P : (u + 1) * P], ident[:])
+            x_words = per_unit.tile([P, TILES, P, 2], F32, align_bytes=64)
+            nc.scalar.copy(out=x_words[:], in_=xt_ps[:].rearrange("p j u r -> p j r u"))
+            live["x_words", unit] = x_words
+
+        def first_matmul(unit):
+            x_words = live.pop(("x_words", unit))
+            x_codes = per_unit.tile([P, UNIT], U32, align_bytes=64)
+            x_scales = per_unit.tile([P, UNIT], U8, align_bytes=64)
+            nc.vector.quantize_mx(
+                out=x_codes[:].bitcast(FP8X4),
+                scales=x_scales[:],
+                in_=x_words[:].rearrange("p j r u -> p (j r u)").bitcast(BF16),
+            )
+            for j in range(TILES):
+                tokens = slice(j * P, (j + 1) * P)
+                h_ps = psum_h.tile([P, H], F32, tag="h_ps")
+                nc.tensor.matmul_mx(
+                    out=h_ps[:],
+                    lhsT=x_codes[:, tokens].bitcast(FP8X4),
+                    lhsT_scale=x_scales[:, tokens],
+                    rhs=w1_codes[:].bitcast(FP8X4),
+                    rhs_scale=w1_scales[:],
+                    start=True,
+                    stop=True,
+                )
+                live["h_ps", unit, j] = h_ps
+
+        def layer_norm(unit):
+            h_sum = per_unit.tile([P, TILES], F32)
+            sq_sum = per_unit.tile([P, TILES], F32)
+            h_tiles = []
+            for j in range(TILES):
+                h = per_tile.tile([P, H], F32)
+                nc.vector.scalar_tensor_tensor(
+                    out=h[:],
+                    in0=live.pop(("h_ps", unit, j))[:],
+                    scalar=1.0,
+                    in1=b1_rows[:],
+                    op0=ALU.mult,
+                    op1=ALU.add,
+                    accum_out=h_sum[:, j : j + 1],
+                )
+                h_tiles.append(h)
+            for j in range(TILES):
+                squares = per_tile.tile([P, H], BF16)
+                nc.scalar.activation(
+                    out=squares[:],
+                    in_=h_tiles[j][:],
+                    func=ACT.Square,
+                    bias=h_sum[:, j : j + 1],
+                    scale=-1.0 * H,
+                    accum_out=sq_sum[:, j : j + 1],
+                )
+            neg_mean = per_unit.tile([P, TILES], F32)
+            nc.gpsimd.tensor_scalar(
+                out=neg_mean[:], in0=h_sum[:], scalar1=-1.0 / H, scalar2=0.0, op0=ALU.mult, op1=ALU.add
+            )
+            var_eps = per_unit.tile([P, TILES], F32)
+            nc.gpsimd.tensor_scalar(
+                out=var_eps[:], in0=sq_sum[:], scalar1=1.0 / (H * H * H), scalar2=EPS, op0=ALU.mult, op1=ALU.add
+            )
+            rstd = per_unit.tile([P, TILES], F32)
+            nc.gpsimd.tensor_tensor(out=rstd[:], in0=var_eps[:], in1=minus_half[:], op=ALU.pow)
+            for j in range(TILES):
+                z = per_tile.tile([P, H], F32)
+                nc.gpsimd.tensor_scalar(
+                    out=z[:],
+                    in0=h_tiles[j][:],
+                    scalar1=neg_mean[:, j : j + 1],
+                    scalar2=rstd[:, j : j + 1],
+                    op0=ALU.add,
+                    op1=ALU.mult,
+                )
+                live["z", unit, j] = z
+
+        def to_features(unit):
+            z_tiles = [live.pop(("z", unit, j)) for j in range(TILES)]
+            r_planes = per_unit.tile([P, PACK, UNIT], BF16)
+            for pair in range(PACK // 2):
+                z_ps = psum_z.tile([P, 2, UNIT], F32)
+                for t2 in range(2):
+                    t = 2 * pair + t2
+                    for j in range(TILES):
+                        nc.tensor.transpose(
+                            z_ps[:, t2, j * P : (j + 1) * P], z_tiles[j][:, t * P : (t + 1) * P], ident[:]
+                        )
+                for t2 in range(2):
+                    t = 2 * pair + t2
+                    nc.scalar.activation(
+                        out=r_planes[:, t, :],
+                        in_=z_ps[:, t2, :],
+                        func=ACT.Relu,
+                        bias=beta_col(t),
+                        scale=gamma_col(t),
+                    )
+            live["r_planes", unit] = r_planes
+
+        def second_matmuls(unit):
+            r_planes = live.pop(("r_planes", unit))
+            r_grouped = per_unit.tile([P, UNIT, PACK], BF16, align_bytes=64)
+            nc.vector.tensor_copy(out=r_grouped[:], in_=r_planes[:].rearrange("p t r -> p r t"))
+            r_codes = per_unit.tile([P, UNIT], U32, align_bytes=64)
+            r_scales = per_unit.tile([P, UNIT], U8, align_bytes=64)
+            nc.vector.quantize_mx(
+                out=r_codes[:].bitcast(FP8X4),
+                scales=r_scales[:],
+                in_=r_grouped[:].rearrange("p r t -> p (r t)"),
+            )
+            w2_codes, w2_scales = w2_q["codes"], w2_q["scales"]
+            x1_ps = psum_a.tile([P, TILES, G], F32)
+            for j in range(TILES):
+                tokens = slice(j * P, (j + 1) * P)
+                nc.tensor.matmul_mx(
+                    out=x1_ps[:, j, :],
+                    lhsT=r_codes[:, tokens].bitcast(FP8X4),
+                    lhsT_scale=r_scales[:, tokens],
+                    rhs=w2_codes[:].bitcast(FP8X4),
+                    rhs_scale=w2_scales[:],
+                    start=True,
+                    stop=True,
+                )
+            x1t_ps = psum_b.tile([P, HALVES, UNIT], F32)
+            for c in range(HALVES):
+                channels = slice(c * P, (c + 1) * P)
+                nc.tensor.matmul_mx(
+                    out=x1t_ps[:, c, :],
+                    lhsT=w2_codes[:, channels].bitcast(FP8X4),
+                    lhsT_scale=w2_scales[:, channels],
+                    rhs=r_codes[:].bitcast(FP8X4),
+                    rhs_scale=r_scales[:],
+                    start=True,
+                    stop=True,
+                )
+            live["x1_ps", unit] = x1_ps
+            live["x1t_ps", unit] = x1t_ps
+
+        def outputs(unit):
+            g, part = divmod(unit, UNITS_PER_GROUP)
+            x1 = per_unit.tile([P, TILES, G], F32)
+            nc.vector.tensor_tensor(
+                out=x1[:],
+                in0=live.pop(("x1_ps", unit))[:],
+                in1=b2_rows[:].unsqueeze(1).to_broadcast([P, TILES, G]),
+                op=ALU.add,
+            )
+            nc.sync.dma_start(
+                out=out_flat[unit * UNIT : (unit + 1) * UNIT, 0:G].rearrange("(j p) c -> p j c", p=P),
+                in_=x1[:],
+            )
+            if part == 0:
+                pooled_new = per_unit.tile([P, HALVES, LINES_PER_GROUP], F32)
+                live["pooled", g] = pooled_new
+            pooled = live["pooled", g]
+            nc.vector.tensor_reduce(
+                out=pooled[:, :, part * LINES_PER_UNIT : (part + 1) * LINES_PER_UNIT],
+                in_=live.pop(("x1t_ps", unit))[:].rearrange("p c (b l) -> p c b l", l=NODES),
+                axis=AXIS.X,
+                op=ALU.max,
+            )
+            if part < UNITS_PER_GROUP - 1:
+                return
+            spread = per_unit.tile([P, HALVES, LINES_PER_GROUP, COPIES], F32)
+            x2_ps = psum_s.tile([P, G], F32, tag="small")
+            for c in range(HALVES):
+                nc.vector.tensor_scalar(
+                    out=spread[:, c, :, :],
+                    in0=pooled[:, c, :].unsqueeze(2).to_broadcast([P, LINES_PER_GROUP, COPIES]),
+                    scalar1=b2_col(c),
+                    scalar2=None,
+                    op0=ALU.add,
+                )
+                nc.tensor.transpose(
+                    x2_ps[:, c * P : (c + 1) * P],
+                    spread[:, c, :, :].rearrange("p b d -> p (b d)"),
+                    ident[:],
+                )
+            x2 = per_unit.tile([P, G], F32)
+            nc.scalar.copy(out=x2[:], in_=x2_ps[:])
+            nc.sync.dma_start(
+                out=out_flat[g * GROUP : (g + 1) * GROUP, G : 2 * G].rearrange(
+                    "(q i) c -> q i c", i=ROWS_PER_COPY
+                ),
+                in_=x2[:].unsqueeze(1).to_broadcast([P, ROWS_PER_COPY, G]),
+            )
+
+        def in_range(unit):
+            return 0 <= unit < N_UNITS
+
+        for k in range(N_UNITS + LAST_LAG):
+            if in_range(k - LAG_SECOND):
+                second_matmuls(k - LAG_SECOND)
+            if in_range(k - LAG_NORM):
+                layer_norm(k - LAG_NORM)
+            if in_range(k - LAG_FEATURES):
+                to_features(k - LAG_FEATURES)
+            if in_range(k):
+                x_to_partitions(k)
+            if in_range(k - LAG_SECOND):
+                outputs(k - LAG_SECOND)
+            if in_range(k - LAG_FIRST):
+                first_matmul(k - LAG_FIRST)
+            if k == LAG_NORM:
+                w2_q["codes"], w2_q["scales"] = quantise_weight(w2_raw, G, "w2")

@@ -31,6 +31,7 @@ LINES_PER_GROUP = GROUP // NODES
 COPIES = P // LINES_PER_GROUP
 ROWS_PER_COPY = NODES // COPIES
 HALVES = G // P
+RUN = 4
 
 LAG_FIRST = 1
 LAG_NORM = 2
@@ -82,8 +83,10 @@ def tile_sub_graph_pa_kernel(tc, x_nodes, w1, b1, gamma, beta, w2, b2, out):
 
         ident = const.tile([P, P], F32)
         make_identity(nc, ident[:])
-        minus_half = const.tile([P, TILES], F32)
-        nc.gpsimd.memset(minus_half[:], -0.5)
+        eps = const.tile([P, 1], F32)
+        nc.vector.memset(eps[:], EPS)
+        warm = const.tile([P, 1], F32)
+        nc.scalar.activation(out=warm[:], in_=eps[:], func=ACT.Abs_reciprocal_sqrt)
 
         bias_in = const.tile([P, H + G], BF16)
         nc.vector.memset(bias_in[:], 0.0)
@@ -99,19 +102,20 @@ def tile_sub_graph_pa_kernel(tc, x_nodes, w1, b1, gamma, beta, w2, b2, out):
 
         rows_f32 = const.tile([P, P], F32)
         nc.vector.tensor_copy(out=rows_f32[:], in_=rows_bf[:])
-        cols_ps = psum_s.tile([P, P], F32, tag="small")
-        nc.tensor.transpose(cols_ps[:], rows_f32[:], ident[:])
         cols = const.tile([P, 16], F32)
-        nc.scalar.copy(out=cols[:], in_=cols_ps[:, 0:16])
-
-        b1_ps = psum_h.tile([P, H], F32, tag="h_ps")
-        nc.tensor.matmul(out=b1_ps[:], lhsT=ones[:], rhs=bias_in[:, 0:H], start=True, stop=True)
         b1_rows = const.tile([P, H], F32)
-        nc.scalar.copy(out=b1_rows[:], in_=b1_ps[:])
-        b2_ps = psum_h.tile([P, H], F32, tag="h_ps")
-        nc.tensor.matmul(out=b2_ps[:, 0:G], lhsT=ones[:], rhs=bias_in[:, H : H + G], start=True, stop=True)
         b2_rows = const.tile([P, G], F32)
-        nc.scalar.copy(out=b2_rows[:], in_=b2_ps[:, 0:G])
+
+        def spread_constants():
+            cols_ps = psum_s.tile([P, P], F32, tag="small")
+            nc.tensor.transpose(cols_ps[:], rows_f32[:], ident[:])
+            nc.scalar.copy(out=cols[:], in_=cols_ps[:, 0:16])
+            b1_ps = psum_h.tile([P, H], F32, tag="h_ps")
+            nc.tensor.matmul(out=b1_ps[:], lhsT=ones[:], rhs=bias_in[:, 0:H], start=True, stop=True)
+            nc.scalar.copy(out=b1_rows[:], in_=b1_ps[:])
+            b2_ps = psum_h.tile([P, H], F32, tag="h_ps")
+            nc.tensor.matmul(out=b2_ps[:, 0:G], lhsT=ones[:], rhs=bias_in[:, H : H + G], start=True, stop=True)
+            nc.scalar.copy(out=b2_rows[:], in_=b2_ps[:, 0:G])
 
         def gamma_col(t):
             return cols[:, t : t + 1]
@@ -124,7 +128,10 @@ def tile_sub_graph_pa_kernel(tc, x_nodes, w1, b1, gamma, beta, w2, b2, out):
 
         def quantise_weight(raw, width, label):
             grouped = const.tile([P, width, PACK], BF16, align_bytes=64, name=label + "_grouped")
-            nc.vector.tensor_copy(out=grouped[:], in_=raw[:].rearrange("p t c -> p c t"))
+            nc.vector.tensor_copy(
+                out=grouped[:].rearrange("p (c i) t -> p c t i", i=RUN),
+                in_=raw[:].rearrange("p t (c i) -> p c t i", i=RUN),
+            )
             codes = const.tile([P, width], U32, align_bytes=64, name=label + "_codes")
             scales = const.tile([P, width], U8, align_bytes=64, name=label + "_scales")
             nc.vector.quantize_mx(
@@ -200,15 +207,11 @@ def tile_sub_graph_pa_kernel(tc, x_nodes, w1, b1, gamma, beta, w2, b2, out):
                     accum_out=sq_sum[:, j : j + 1],
                 )
             neg_mean = per_unit.tile([P, TILES], F32)
-            nc.gpsimd.tensor_scalar(
-                out=neg_mean[:], in0=h_sum[:], scalar1=-1.0 / H, scalar2=0.0, op0=ALU.mult, op1=ALU.add
-            )
-            var_eps = per_unit.tile([P, TILES], F32)
-            nc.gpsimd.tensor_scalar(
-                out=var_eps[:], in0=sq_sum[:], scalar1=1.0 / (H * H * H), scalar2=EPS, op0=ALU.mult, op1=ALU.add
-            )
+            nc.scalar.mul(out=neg_mean[:], in_=h_sum[:], mul=-1.0 / H)
             rstd = per_unit.tile([P, TILES], F32)
-            nc.gpsimd.tensor_tensor(out=rstd[:], in0=var_eps[:], in1=minus_half[:], op=ALU.pow)
+            nc.scalar.activation(
+                out=rstd[:], in_=sq_sum[:], func=ACT.Abs_reciprocal_sqrt, bias=eps[:], scale=1.0 / (H * H * H)
+            )
             for j in range(TILES):
                 z = per_tile.tile([P, H], F32)
                 nc.gpsimd.tensor_scalar(
@@ -224,29 +227,32 @@ def tile_sub_graph_pa_kernel(tc, x_nodes, w1, b1, gamma, beta, w2, b2, out):
         def to_features(unit):
             z_tiles = [live.pop(("z", unit, j)) for j in range(TILES)]
             r_planes = per_unit.tile([P, PACK, UNIT], BF16)
+            z_banks = []
             for pair in range(PACK // 2):
                 z_ps = psum_z.tile([P, 2, UNIT], F32)
-                for t2 in range(2):
-                    t = 2 * pair + t2
-                    for j in range(TILES):
-                        nc.tensor.transpose(
-                            z_ps[:, t2, j * P : (j + 1) * P], z_tiles[j][:, t * P : (t + 1) * P], ident[:]
-                        )
-                for t2 in range(2):
-                    t = 2 * pair + t2
-                    nc.scalar.activation(
-                        out=r_planes[:, t, :],
-                        in_=z_ps[:, t2, :],
-                        func=ACT.Relu,
-                        bias=beta_col(t),
-                        scale=gamma_col(t),
+                z_banks.append(z_ps)
+            for j in range(TILES):
+                for t in range(PACK):
+                    nc.tensor.transpose(
+                        z_banks[t // 2][:, t % 2, j * P : (j + 1) * P], z_tiles[j][:, t * P : (t + 1) * P], ident[:]
                     )
+            for t in range(PACK):
+                nc.scalar.activation(
+                    out=r_planes[:, t, :],
+                    in_=z_banks[t // 2][:, t % 2, :],
+                    func=ACT.Relu,
+                    bias=beta_col(t),
+                    scale=gamma_col(t),
+                )
             live["r_planes", unit] = r_planes
 
         def second_matmuls(unit):
             r_planes = live.pop(("r_planes", unit))
             r_grouped = per_unit.tile([P, UNIT, PACK], BF16, align_bytes=64)
-            nc.vector.tensor_copy(out=r_grouped[:], in_=r_planes[:].rearrange("p t r -> p r t"))
+            nc.vector.tensor_copy(
+                out=r_grouped[:].rearrange("p (c i) t -> p c t i", i=RUN),
+                in_=r_planes[:].rearrange("p t (c i) -> p c t i", i=RUN),
+            )
             r_codes = per_unit.tile([P, UNIT], U32, align_bytes=64)
             r_scales = per_unit.tile([P, UNIT], U8, align_bytes=64)
             nc.vector.quantize_mx(
@@ -343,6 +349,8 @@ def tile_sub_graph_pa_kernel(tc, x_nodes, w1, b1, gamma, beta, w2, b2, out):
                 to_features(k - LAG_FEATURES)
             if in_range(k):
                 x_to_partitions(k)
+            if k == 0:
+                spread_constants()
             if in_range(k - LAG_SECOND):
                 outputs(k - LAG_SECOND)
             if in_range(k - LAG_FIRST):

@@ -33,11 +33,7 @@ ROWS_PER_COPY = NODES // COPIES
 HALVES = G // P
 RUN = 4
 
-LAG_FIRST = 1
-LAG_NORM = 2
-LAG_FEATURES = 3
-LAG_SECOND = 5
-LAST_LAG = LAG_SECOND
+N_STAGES = 8
 
 FLOPS = 2 * TOKENS * H * H + 2 * TOKENS * H * G
 
@@ -246,7 +242,7 @@ def tile_sub_graph_pa_kernel(tc, x_nodes, w1, b1, gamma, beta, w2, b2, out):
                 )
             live["r_planes", unit] = r_planes
 
-        def second_matmuls(unit):
+        def quantise_r(unit):
             r_planes = live.pop(("r_planes", unit))
             r_grouped = per_unit.tile([P, UNIT, PACK], BF16, align_bytes=64)
             nc.vector.tensor_copy(
@@ -260,6 +256,12 @@ def tile_sub_graph_pa_kernel(tc, x_nodes, w1, b1, gamma, beta, w2, b2, out):
                 scales=r_scales[:],
                 in_=r_grouped[:].rearrange("p r t -> p (r t)"),
             )
+            live["r_codes", unit] = r_codes
+            live["r_scales", unit] = r_scales
+
+        def second_matmuls(unit):
+            r_codes = live.pop(("r_codes", unit))
+            r_scales = live.pop(("r_scales", unit))
             w2_codes, w2_scales = w2_q["codes"], w2_q["scales"]
             x1_ps = psum_a.tile([P, TILES, G], F32)
             for j in range(TILES):
@@ -311,8 +313,12 @@ def tile_sub_graph_pa_kernel(tc, x_nodes, w1, b1, gamma, beta, w2, b2, out):
                 axis=AXIS.X,
                 op=ALU.max,
             )
+
+        def pool(unit):
+            g, part = divmod(unit, UNITS_PER_GROUP)
             if part < UNITS_PER_GROUP - 1:
                 return
+            pooled = live.pop(("pooled", g))
             spread = per_unit.tile([P, HALVES, LINES_PER_GROUP, COPIES], F32)
             x2_ps = psum_s.tile([P, G], F32, tag="small")
             for c in range(HALVES):
@@ -337,23 +343,32 @@ def tile_sub_graph_pa_kernel(tc, x_nodes, w1, b1, gamma, beta, w2, b2, out):
                 in_=x2[:].unsqueeze(1).to_broadcast([P, ROWS_PER_COPY, G]),
             )
 
-        def in_range(unit):
-            return 0 <= unit < N_UNITS
+        stage_of = {
+            "x_to_partitions": 0,
+            "first_matmul": 1,
+            "layer_norm": 2,
+            "to_features": 3,
+            "quantise_r": 4,
+            "second_matmuls": 5,
+            "outputs": 6,
+            "pool": 7,
+        }
 
-        for k in range(N_UNITS + LAST_LAG):
-            if in_range(k - LAG_SECOND):
-                second_matmuls(k - LAG_SECOND)
-            if in_range(k - LAG_NORM):
-                layer_norm(k - LAG_NORM)
-            if in_range(k - LAG_FEATURES):
-                to_features(k - LAG_FEATURES)
-            if in_range(k):
-                x_to_partitions(k)
+        def run(stage, name, k):
+            unit = k - stage_of[name]
+            if 0 <= unit < N_UNITS:
+                stage(unit)
+
+        for k in range(N_UNITS + N_STAGES - 1):
+            run(outputs, "outputs", k)
+            run(second_matmuls, "second_matmuls", k)
+            run(layer_norm, "layer_norm", k)
+            run(to_features, "to_features", k)
+            run(first_matmul, "first_matmul", k)
+            run(quantise_r, "quantise_r", k)
+            run(x_to_partitions, "x_to_partitions", k)
+            run(pool, "pool", k)
             if k == 0:
                 spread_constants()
-            if in_range(k - LAG_SECOND):
-                outputs(k - LAG_SECOND)
-            if in_range(k - LAG_FIRST):
-                first_matmul(k - LAG_FIRST)
-            if k == LAG_NORM:
+            if k == stage_of["to_features"]:
                 w2_q["codes"], w2_q["scales"] = quantise_weight(w2_raw, G, "w2")

@@ -33,7 +33,15 @@ ROWS_PER_COPY = NODES // COPIES
 HALVES = G // P
 RUN = 4
 
-N_STAGES = 8
+S_TRANSPOSE_X = 0
+S_COPY_X = 1
+S_FIRST = 2
+S_NORM = 3
+S_FEATURES = 4
+S_QUANTISE_R = 5
+S_SECOND = 6
+S_OUTPUTS = 7
+S_POOL = 8
 
 FLOPS = 2 * TOKENS * H * H + 2 * TOKENS * H * G
 
@@ -141,19 +149,29 @@ def tile_sub_graph_pa_kernel(tc, x_nodes, w1, b1, gamma, beta, w2, b2, out):
         w2_q = {}
 
         live = {}
+        units = range(N_UNITS)
 
-        def x_to_partitions(unit):
+        def transpose_x(unit):
+            if unit not in units:
+                return
             g, part = divmod(unit, UNITS_PER_GROUP)
             xt_ps = psum_x.tile([P, TILES, 2, P], F32)
             for j in range(TILES):
                 words = x_tiles[g][:, part * TILES + j, :].bitcast(F32)
                 for u in range(2):
                     nc.tensor.transpose(xt_ps[:, j, u, :], words[:, u * P : (u + 1) * P], ident[:])
+            live["xt_ps", unit] = xt_ps
+
+        def copy_x(unit):
+            if unit not in units:
+                return
             x_words = per_unit.tile([P, TILES, P, 2], F32, align_bytes=64)
-            nc.scalar.copy(out=x_words[:], in_=xt_ps[:].rearrange("p j u r -> p j r u"))
+            nc.scalar.copy(out=x_words[:], in_=live.pop(("xt_ps", unit))[:].rearrange("p j u r -> p j r u"))
             live["x_words", unit] = x_words
 
         def first_matmul(unit):
+            if unit not in units:
+                return
             x_words = live.pop(("x_words", unit))
             x_codes = per_unit.tile([P, UNIT], U32, align_bytes=64)
             x_scales = per_unit.tile([P, UNIT], U8, align_bytes=64)
@@ -176,7 +194,9 @@ def tile_sub_graph_pa_kernel(tc, x_nodes, w1, b1, gamma, beta, w2, b2, out):
                 )
                 live["h_ps", unit, j] = h_ps
 
-        def layer_norm(unit):
+        def bias_and_squares(unit):
+            if unit not in units:
+                return
             h_sum = per_unit.tile([P, TILES], F32)
             sq_sum = per_unit.tile([P, TILES], F32)
             h_tiles = []
@@ -202,6 +222,16 @@ def tile_sub_graph_pa_kernel(tc, x_nodes, w1, b1, gamma, beta, w2, b2, out):
                     scale=-1.0 * H,
                     accum_out=sq_sum[:, j : j + 1],
                 )
+            live["h", unit] = h_tiles
+            live["h_sum", unit] = h_sum
+            live["sq_sum", unit] = sq_sum
+
+        def normalise(unit):
+            if unit not in units:
+                return
+            h_tiles = live.pop(("h", unit))
+            h_sum = live.pop(("h_sum", unit))
+            sq_sum = live.pop(("sq_sum", unit))
             neg_mean = per_unit.tile([P, TILES], F32)
             nc.scalar.mul(out=neg_mean[:], in_=h_sum[:], mul=-1.0 / H)
             rstd = per_unit.tile([P, TILES], F32)
@@ -221,6 +251,8 @@ def tile_sub_graph_pa_kernel(tc, x_nodes, w1, b1, gamma, beta, w2, b2, out):
                 live["z", unit, j] = z
 
         def to_features(unit):
+            if unit not in units:
+                return
             z_tiles = [live.pop(("z", unit, j)) for j in range(TILES)]
             r_planes = per_unit.tile([P, PACK, UNIT], BF16)
             z_banks = []
@@ -242,13 +274,21 @@ def tile_sub_graph_pa_kernel(tc, x_nodes, w1, b1, gamma, beta, w2, b2, out):
                 )
             live["r_planes", unit] = r_planes
 
-        def quantise_r(unit):
+        def regroup_r(unit):
+            if unit not in units:
+                return
             r_planes = live.pop(("r_planes", unit))
             r_grouped = per_unit.tile([P, UNIT, PACK], BF16, align_bytes=64)
             nc.vector.tensor_copy(
                 out=r_grouped[:].rearrange("p (c i) t -> p c t i", i=RUN),
                 in_=r_planes[:].rearrange("p t (c i) -> p c t i", i=RUN),
             )
+            live["r_grouped", unit] = r_grouped
+
+        def quantise_r(unit):
+            if unit not in units:
+                return
+            r_grouped = live.pop(("r_grouped", unit))
             r_codes = per_unit.tile([P, UNIT], U32, align_bytes=64)
             r_scales = per_unit.tile([P, UNIT], U8, align_bytes=64)
             nc.vector.quantize_mx(
@@ -260,6 +300,8 @@ def tile_sub_graph_pa_kernel(tc, x_nodes, w1, b1, gamma, beta, w2, b2, out):
             live["r_scales", unit] = r_scales
 
         def second_matmuls(unit):
+            if unit not in units:
+                return
             r_codes = live.pop(("r_codes", unit))
             r_scales = live.pop(("r_scales", unit))
             w2_codes, w2_scales = w2_q["codes"], w2_q["scales"]
@@ -291,6 +333,8 @@ def tile_sub_graph_pa_kernel(tc, x_nodes, w1, b1, gamma, beta, w2, b2, out):
             live["x1t_ps", unit] = x1t_ps
 
         def outputs(unit):
+            if unit not in units:
+                return
             g, part = divmod(unit, UNITS_PER_GROUP)
             x1 = per_unit.tile([P, TILES, G], F32)
             nc.vector.tensor_tensor(
@@ -316,7 +360,7 @@ def tile_sub_graph_pa_kernel(tc, x_nodes, w1, b1, gamma, beta, w2, b2, out):
 
         def pool(unit):
             g, part = divmod(unit, UNITS_PER_GROUP)
-            if part < UNITS_PER_GROUP - 1:
+            if unit not in units or part < UNITS_PER_GROUP - 1:
                 return
             pooled = live.pop(("pooled", g))
             spread = per_unit.tile([P, HALVES, LINES_PER_GROUP, COPIES], F32)
@@ -343,32 +387,19 @@ def tile_sub_graph_pa_kernel(tc, x_nodes, w1, b1, gamma, beta, w2, b2, out):
                 in_=x2[:].unsqueeze(1).to_broadcast([P, ROWS_PER_COPY, G]),
             )
 
-        stage_of = {
-            "x_to_partitions": 0,
-            "first_matmul": 1,
-            "layer_norm": 2,
-            "to_features": 3,
-            "quantise_r": 4,
-            "second_matmuls": 5,
-            "outputs": 6,
-            "pool": 7,
-        }
-
-        def run(stage, name, k):
-            unit = k - stage_of[name]
-            if 0 <= unit < N_UNITS:
-                stage(unit)
-
-        for k in range(N_UNITS + N_STAGES - 1):
-            run(outputs, "outputs", k)
-            run(second_matmuls, "second_matmuls", k)
-            run(layer_norm, "layer_norm", k)
-            run(to_features, "to_features", k)
-            run(first_matmul, "first_matmul", k)
-            run(quantise_r, "quantise_r", k)
-            run(x_to_partitions, "x_to_partitions", k)
-            run(pool, "pool", k)
-            if k == 0:
+        for k in range(N_UNITS + S_POOL):
+            outputs(k - S_OUTPUTS)
+            second_matmuls(k - S_SECOND)
+            bias_and_squares(k - S_NORM)
+            copy_x(k - S_COPY_X)
+            normalise(k - S_NORM)
+            to_features(k - S_FEATURES)
+            regroup_r(k - S_QUANTISE_R)
+            first_matmul(k - S_FIRST)
+            pool(k - S_POOL)
+            quantise_r(k - S_QUANTISE_R)
+            transpose_x(k - S_TRANSPOSE_X)
+            if k == S_TRANSPOSE_X:
                 spread_constants()
-            if k == stage_of["to_features"]:
+            if k == S_FEATURES:
                 w2_q["codes"], w2_q["scales"] = quantise_weight(w2_raw, G, "w2")

@@ -31,6 +31,7 @@ LINES_PER_GROUP = GROUP // NODES
 COPIES = P // LINES_PER_GROUP
 ROWS_PER_COPY = NODES // COPIES
 HALVES = G // P
+FIRST_PASSES = 2
 RUN = 4
 
 S_TRANSPOSE_X = 0
@@ -183,15 +184,16 @@ def tile_sub_graph_pa_kernel(tc, x_nodes, w1, b1, gamma, beta, w2, b2, out):
             for j in range(TILES):
                 tokens = slice(j * P, (j + 1) * P)
                 h_ps = psum_h.tile([P, H], F32, tag="h_ps")
-                nc.tensor.matmul_mx(
-                    out=h_ps[:],
-                    lhsT=x_codes[:, tokens].bitcast(FP8X4),
-                    lhsT_scale=x_scales[:, tokens],
-                    rhs=w1_codes[:].bitcast(FP8X4),
-                    rhs_scale=w1_scales[:],
-                    start=True,
-                    stop=True,
-                )
+                for repeat in range(FIRST_PASSES):
+                    nc.tensor.matmul_mx(
+                        out=h_ps[:],
+                        lhsT=x_codes[:, tokens].bitcast(FP8X4),
+                        lhsT_scale=x_scales[:, tokens],
+                        rhs=w1_codes[:].bitcast(FP8X4),
+                        rhs_scale=w1_scales[:],
+                        start=True,
+                        stop=True,
+                    )
                 live["h_ps", unit, j] = h_ps
 
         def bias_and_squares(unit):

@@ -25,13 +25,11 @@ UNIT = TILES * P
 N_UNITS = TOKENS // UNIT
 UNITS_PER_GROUP = 2
 GROUP = UNITS_PER_GROUP * UNIT
-N_GROUPS = TOKENS // GROUP
 LINES_PER_UNIT = UNIT // NODES
 LINES_PER_GROUP = GROUP // NODES
 COPIES = P // LINES_PER_GROUP
 ROWS_PER_COPY = NODES // COPIES
 HALVES = G // P
-FIRST_PASSES = 2
 RUN = 4
 
 S_TRANSPOSE_X = 0
@@ -70,21 +68,21 @@ def tile_sub_graph_pa_kernel(tc, x_nodes, w1, b1, gamma, beta, w2, b2, out):
             in_=w1.rearrange("(u q e) c -> q u e c", u=2, e=2),
         )
         x_tiles = []
-        for g in range(N_GROUPS):
-            x_sb = const.tile([P, GROUP // P, H], BF16, name="x_sb%d" % g)
+        for unit in range(N_UNITS):
+            x_sb = const.tile([P, TILES, H], BF16, name="x_sb%d" % unit)
             x_tiles.append(x_sb)
 
-        def load_x(g):
+        def load_x(unit):
             nc.sync.dma_start(
-                out=x_tiles[g][:],
-                in_=x_flat[g * GROUP : (g + 1) * GROUP, :].rearrange("(j p) k -> p j k", p=P),
+                out=x_tiles[unit][:],
+                in_=x_flat[unit * UNIT : (unit + 1) * UNIT, :].rearrange("(j p) k -> p j k", p=P),
             )
 
         load_x(0)
         w2_raw = const.tile([P, PACK, G], BF16)
         nc.sync.dma_start(out=w2_raw[:], in_=w2.rearrange("(t p) n -> p t n", p=P))
-        for g in range(1, N_GROUPS):
-            load_x(g)
+        for unit in range(1, N_UNITS):
+            load_x(unit)
 
         ident = const.tile([P, P], F32)
         make_identity(nc, ident[:])
@@ -155,10 +153,9 @@ def tile_sub_graph_pa_kernel(tc, x_nodes, w1, b1, gamma, beta, w2, b2, out):
         def transpose_x(unit):
             if unit not in units:
                 return
-            g, part = divmod(unit, UNITS_PER_GROUP)
             xt_ps = psum_x.tile([P, TILES, 2, P], F32)
             for j in range(TILES):
-                words = x_tiles[g][:, part * TILES + j, :].bitcast(F32)
+                words = x_tiles[unit][:, j, :].bitcast(F32)
                 for u in range(2):
                     nc.tensor.transpose(xt_ps[:, j, u, :], words[:, u * P : (u + 1) * P], ident[:])
             live["xt_ps", unit] = xt_ps
@@ -184,16 +181,15 @@ def tile_sub_graph_pa_kernel(tc, x_nodes, w1, b1, gamma, beta, w2, b2, out):
             for j in range(TILES):
                 tokens = slice(j * P, (j + 1) * P)
                 h_ps = psum_h.tile([P, H], F32, tag="h_ps")
-                for repeat in range(FIRST_PASSES):
-                    nc.tensor.matmul_mx(
-                        out=h_ps[:],
-                        lhsT=x_codes[:, tokens].bitcast(FP8X4),
-                        lhsT_scale=x_scales[:, tokens],
-                        rhs=w1_codes[:].bitcast(FP8X4),
-                        rhs_scale=w1_scales[:],
-                        start=True,
-                        stop=True,
-                    )
+                nc.tensor.matmul_mx(
+                    out=h_ps[:],
+                    lhsT=x_codes[:, tokens].bitcast(FP8X4),
+                    lhsT_scale=x_scales[:, tokens],
+                    rhs=w1_codes[:].bitcast(FP8X4),
+                    rhs_scale=w1_scales[:],
+                    start=True,
+                    stop=True,
+                )
                 live["h_ps", unit, j] = h_ps
 
         def bias_and_squares(unit):
@@ -401,7 +397,7 @@ def tile_sub_graph_pa_kernel(tc, x_nodes, w1, b1, gamma, beta, w2, b2, out):
             pool(k - S_POOL)
             quantise_r(k - S_QUANTISE_R)
             transpose_x(k - S_TRANSPOSE_X)
-            if k == S_TRANSPOSE_X:
+            if k == S_COPY_X:
                 spread_constants()
             if k == S_FEATURES:
                 w2_q["codes"], w2_q["scales"] = quantise_weight(w2_raw, G, "w2")

from contextlib import ExitStack

import concourse.mybir as mybir
from concourse.masks import make_identity

F32 = mybir.dt.float32
BF16 = mybir.dt.bfloat16
U32 = mybir.dt.uint32
U8 = mybir.dt.uint8
FP8X4 = mybir.dt.float8_e4m3fn_x4
ALU = mybir.AluOpType
ACT = mybir.ActivationFunctionType
AXIS = mybir.AxisListType

P = 128
PACK = 4
TOKENS = 64 * 64
NODES = 64
H = 512
G = 256
EPS = 1e-5

TILES = 2
UNIT = TILES * P
N_UNITS = TOKENS // UNIT
UNITS_PER_GROUP = 2
GROUP = UNITS_PER_GROUP * UNIT
LINES_PER_UNIT = UNIT // NODES
LINES_PER_GROUP = GROUP // NODES
COPIES = P // LINES_PER_GROUP
ROWS_PER_COPY = NODES // COPIES
HALVES = G // P
RUN = 4

S_TRANSPOSE_X = 0
S_COPY_X = 1
S_FIRST = 2
S_NORM = 3
S_FEATURES = 4
S_QUANTISE_R = 5
S_SECOND = 6
S_OUTPUTS = 7
S_POOL = 8

FLOPS = 2 * TOKENS * H * H + 2 * TOKENS * H * G


def tile_sub_graph_pa_kernel(tc, x_nodes, w1, b1, gamma, beta, w2, b2, out):
    nc = tc.nc
    x_flat = x_nodes.flatten_outer_dims()
    out_flat = out.flatten_outer_dims()

    with ExitStack() as ctx:
        ctx.enter_context(tc.manual_schedule())
        const = ctx.enter_context(tc.tile_pool(name="const", bufs=1))
        per_unit = ctx.enter_context(tc.tile_pool(name="per_unit", bufs=4))
        per_tile = ctx.enter_context(tc.tile_pool(name="per_tile", bufs=4 * TILES))
        psum_x = ctx.enter_context(tc.psum_pool(name="psum_x", bufs=1))
        psum_h = ctx.enter_context(tc.psum_pool(name="psum_h", bufs=2))
        psum_z = ctx.enter_context(tc.psum_pool(name="psum_z", bufs=2))
        psum_a = ctx.enter_context(tc.psum_pool(name="psum_a", bufs=1))
        psum_b = ctx.enter_context(tc.psum_pool(name="psum_b", bufs=1))
        psum_s = ctx.enter_context(tc.psum_pool(name="psum_s", bufs=1))

        w1_raw = const.tile([P, PACK, H], BF16)
        nc.sync.dma_start(
            out=w1_raw[:].rearrange("q (u e) c -> q u e c", u=2),
            in_=w1.rearrange("(u q e) c -> q u e c", u=2, e=2),
        )
        x_tiles = []
        for unit in range(N_UNITS):
            x_sb = const.tile([P, TILES, H], BF16, name="x_sb%d" % unit)
            x_tiles.append(x_sb)

        def load_x(unit):
            nc.sync.dma_start(
                out=x_tiles[unit][:],
                in_=x_flat[unit * UNIT : (unit + 1) * UNIT, :].rearrange("(j p) k -> p j k", p=P),
            )

        load_x(0)
        w2_raw = const.tile([P, PACK, G], BF16)
        nc.sync.dma_start(out=w2_raw[:], in_=w2.rearrange("(t p) n -> p t n", p=P))
        for unit in range(1, N_UNITS):
            load_x(unit)

        ident = const.tile([P, P], F32)
        make_identity(nc, ident[:])
        eps = const.tile([P, 1], F32)
        nc.vector.memset(eps[:], EPS)
        warm = const.tile([P, 1], F32)
        nc.scalar.activation(out=warm[:], in_=eps[:], func=ACT.Abs_reciprocal_sqrt)

        bias_in = const.tile([P, H + G], BF16)
        nc.vector.memset(bias_in[:], 0.0)
        nc.scalar.dma_start(out=bias_in[0:1, 0:H], in_=b1.rearrange("(o k) -> o k", o=1))
        nc.scalar.dma_start(out=bias_in[0:1, H : H + G], in_=b2.rearrange("(o k) -> o k", o=1))
        ones = const.tile([P, P], BF16)
        nc.vector.memset(ones[:], 1.0)
        rows_bf = const.tile([P, P], BF16)
        nc.vector.memset(rows_bf[:], 0.0)
        nc.scalar.dma_start(out=rows_bf[0:4, :], in_=gamma.rearrange("(t p) -> t p", p=P))
        nc.scalar.dma_start(out=rows_bf[4:8, :], in_=beta.rearrange("(t p) -> t p", p=P))
        nc.scalar.dma_start(out=rows_bf[8:10, :], in_=b2.rearrange("(t p) -> t p", p=P))

        rows_f32 = const.tile([P, P], F32)
        nc.vector.tensor_copy(out=rows_f32[:], in_=rows_bf[:])
        cols = const.tile([P, 16], F32)
        b1_rows = const.tile([P, H], F32)
        b2_rows = const.tile([P, G], F32)

        def spread_constants():
            cols_ps = psum_s.tile([P, P], F32, tag="small")
            nc.tensor.transpose(cols_ps[:], rows_f32[:], ident[:])
            nc.scalar.copy(out=cols[:], in_=cols_ps[:, 0:16])
            b1_ps = psum_h.tile([P, H], F32, tag="h_ps")
            nc.tensor.matmul(out=b1_ps[:], lhsT=ones[:], rhs=bias_in[:, 0:H], start=True, stop=True)
            nc.scalar.copy(out=b1_rows[:], in_=b1_ps[:])
            b2_ps = psum_h.tile([P, H], F32, tag="h_ps")
            nc.tensor.matmul(out=b2_ps[:, 0:G], lhsT=ones[:], rhs=bias_in[:, H : H + G], start=True, stop=True)
            nc.scalar.copy(out=b2_rows[:], in_=b2_ps[:, 0:G])

        def gamma_col(t):
            return cols[:, t : t + 1]

        def beta_col(t):
            return cols[:, 4 + t : 5 + t]

        def b2_col(c):
            return cols[:, 8 + c : 9 + c]

        def quantise_weight(raw, width, label):
            grouped = const.tile([P, width, PACK], BF16, align_bytes=64, name=label + "_grouped")
            nc.vector.tensor_copy(
                out=grouped[:].rearrange("p (c i) t -> p c t i", i=RUN),
                in_=raw[:].rearrange("p t (c i) -> p c t i", i=RUN),
            )
            codes = const.tile([P, width], U32, align_bytes=64, name=label + "_codes")
            scales = const.tile([P, width], U8, align_bytes=64, name=label + "_scales")
            nc.vector.quantize_mx(
                out=codes[:].bitcast(FP8X4),
                scales=scales[:],
                in_=grouped[:].rearrange("p c t -> p (c t)"),
            )
            return codes, scales

        w1_codes, w1_scales = quantise_weight(w1_raw, H, "w1")
        w2_q = {}

        live = {}
        units = range(N_UNITS)

        def transpose_x(unit):
            if unit not in units:
                return
            xt_ps = psum_x.tile([P, TILES, 2, P], F32)
            for j in range(TILES):
                words = x_tiles[unit][:, j, :].bitcast(F32)
                for u in range(2):
                    nc.tensor.transpose(xt_ps[:, j, u, :], words[:, u * P : (u + 1) * P], ident[:])
            live["xt_ps", unit] = xt_ps

        def copy_x(unit):
            if unit not in units:
                return
            x_words = per_unit.tile([P, TILES, P, 2], F32, align_bytes=64)
            nc.scalar.copy(out=x_words[:], in_=live.pop(("xt_ps", unit))[:].rearrange("p j u r -> p j r u"))
            live["x_words", unit] = x_words

        def first_matmul(unit):
            if unit not in units:
                return
            x_words = live.pop(("x_words", unit))
            x_codes = per_unit.tile([P, UNIT], U32, align_bytes=64)
            x_scales = per_unit.tile([P, UNIT], U8, align_bytes=64)
            nc.vector.quantize_mx(
                out=x_codes[:].bitcast(FP8X4),
                scales=x_scales[:],
                in_=x_words[:].rearrange("p j r u -> p (j r u)").bitcast(BF16),
            )
            for j in range(TILES):
                tokens = slice(j * P, (j + 1) * P)
                h_ps = psum_h.tile([P, H], F32, tag="h_ps")
                nc.tensor.matmul_mx(
                    out=h_ps[:],
                    lhsT=x_codes[:, tokens].bitcast(FP8X4),
                    lhsT_scale=x_scales[:, tokens],
                    rhs=w1_codes[:].bitcast(FP8X4),
                    rhs_scale=w1_scales[:],
                    start=True,
                    stop=True,
                )
                live["h_ps", unit, j] = h_ps

        def bias_and_squares(unit):
            if unit not in units:
                return
            h_sum = per_unit.tile([P, TILES], F32)
            sq_sum = per_unit.tile([P, TILES], F32)
            h_tiles = []
            for j in range(TILES):
                h = per_tile.tile([P, H], F32)
                nc.vector.scalar_tensor_tensor(
                    out=h[:],
                    in0=live.pop(("h_ps", unit, j))[:],
                    scalar=1.0,
                    in1=b1_rows[:],
                    op0=ALU.mult,
                    op1=ALU.add,
                    accum_out=h_sum[:, j : j + 1],
                )
                h_tiles.append(h)
            for j in range(TILES):
                squares = per_tile.tile([P, H], BF16)
                nc.scalar.activation(
                    out=squares[:],
                    in_=h_tiles[j][:],
                    func=ACT.Square,
                    bias=h_sum[:, j : j + 1],
                    scale=-1.0 * H,
                    accum_out=sq_sum[:, j : j + 1],
                )
            live["h", unit] = h_tiles
            live["h_sum", unit] = h_sum
            live["sq_sum", unit] = sq_sum

        def normalise(unit):
            if unit not in units:
                return
            h_tiles = live.pop(("h", unit))
            h_sum = live.pop(("h_sum", unit))
            sq_sum = live.pop(("sq_sum", unit))
            neg_mean = per_unit.tile([P, TILES], F32)
            nc.scalar.mul(out=neg_mean[:], in_=h_sum[:], mul=-1.0 / H)
            rstd = per_unit.tile([P, TILES], F32)
            nc.scalar.activation(
                out=rstd[:], in_=sq_sum[:], func=ACT.Abs_reciprocal_sqrt, bias=eps[:], scale=1.0 / (H * H * H)
            )
            for j in range(TILES):
                z = per_tile.tile([P, H], F32)
                nc.gpsimd.tensor_scalar(
                    out=z[:],
                    in0=h_tiles[j][:],
                    scalar1=neg_mean[:, j : j + 1],
                    scalar2=rstd[:, j : j + 1],
                    op0=ALU.add,
                    op1=ALU.mult,
                )
                live["z", unit, j] = z

        def to_features(unit):
            if unit not in units:
                return
            z_tiles = [live.pop(("z", unit, j)) for j in range(TILES)]
            r_planes = per_unit.tile([P, PACK, UNIT], BF16)
            z_banks = []
            for pair in range(PACK // 2):
                z_ps = psum_z.tile([P, 2, UNIT], F32)
                z_banks.append(z_ps)
            for j in range(TILES):
                for t in range(PACK):
                    nc.tensor.transpose(
                        z_banks[t // 2][:, t % 2, j * P : (j + 1) * P], z_tiles[j][:, t * P : (t + 1) * P], ident[:]
                    )
            for t in range(PACK):
                nc.scalar.activation(
                    out=r_planes[:, t, :],
                    in_=z_banks[t // 2][:, t % 2, :],
                    func=ACT.Relu,
                    bias=beta_col(t),
                    scale=gamma_col(t),
                )
            live["r_planes", unit] = r_planes

        def regroup_r(unit):
            if unit not in units:
                return
            r_planes = live.pop(("r_planes", unit))
            r_grouped = per_unit.tile([P, UNIT, PACK], BF16, align_bytes=64)
            nc.vector.tensor_copy(
                out=r_grouped[:].rearrange("p (c i) t -> p c t i", i=RUN),
                in_=r_planes[:].rearrange("p t (c i) -> p c t i", i=RUN),
            )
            live["r_grouped", unit] = r_grouped

        def quantise_r(unit):
            if unit not in units:
                return
            r_grouped = live.pop(("r_grouped", unit))
            r_codes = per_unit.tile([P, UNIT], U32, align_bytes=64)
            r_scales = per_unit.tile([P, UNIT], U8, align_bytes=64)
            nc.vector.quantize_mx(
                out=r_codes[:].bitcast(FP8X4),
                scales=r_scales[:],
                in_=r_grouped[:].rearrange("p r t -> p (r t)"),
            )
            live["r_codes", unit] = r_codes
            live["r_scales", unit] = r_scales

        def second_matmuls(unit):
            if unit not in units:
                return
            r_codes = live.pop(("r_codes", unit))
            r_scales = live.pop(("r_scales", unit))
            w2_codes, w2_scales = w2_q["codes"], w2_q["scales"]
            x1_ps = psum_a.tile([P, TILES, G], F32)
            for j in range(TILES):
                tokens = slice(j * P, (j + 1) * P)
                nc.tensor.matmul_mx(
                    out=x1_ps[:, j, :],
                    lhsT=r_codes[:, tokens].bitcast(FP8X4),
                    lhsT_scale=r_scales[:, tokens],
                    rhs=w2_codes[:].bitcast(FP8X4),
                    rhs_scale=w2_scales[:],
                    start=True,
                    stop=True,
                )
            x1t_ps = psum_b.tile([P, HALVES, UNIT], F32)
            for c in range(HALVES):
                channels = slice(c * P, (c + 1) * P)
                nc.tensor.matmul_mx(
                    out=x1t_ps[:, c, :],
                    lhsT=w2_codes[:, channels].bitcast(FP8X4),
                    lhsT_scale=w2_scales[:, channels],
                    rhs=r_codes[:].bitcast(FP8X4),
                    rhs_scale=r_scales[:],
                    start=True,
                    stop=True,
                )
            live["x1_ps", unit] = x1_ps
            live["x1t_ps", unit] = x1t_ps

        def outputs(unit):
            if unit not in units:
                return
            g, part = divmod(unit, UNITS_PER_GROUP)
            x1 = per_unit.tile([P, TILES, G], F32)
            nc.vector.tensor_tensor(
                out=x1[:],
                in0=live.pop(("x1_ps", unit))[:],
                in1=b2_rows[:].unsqueeze(1).to_broadcast([P, TILES, G]),
                op=ALU.add,
            )
            nc.sync.dma_start(
                out=out_flat[unit * UNIT : (unit + 1) * UNIT, 0:G].rearrange("(j p) c -> p j c", p=P),
                in_=x1[:],
            )
            if part == 0:
                pooled_new = per_unit.tile([P, HALVES, LINES_PER_GROUP], F32)
                live["pooled", g] = pooled_new
            pooled = live["pooled", g]
            nc.vector.tensor_reduce(
                out=pooled[:, :, part * LINES_PER_UNIT : (part + 1) * LINES_PER_UNIT],
                in_=live.pop(("x1t_ps", unit))[:].rearrange("p c (b l) -> p c b l", l=NODES),
                axis=AXIS.X,
                op=ALU.max,
            )

        def pool(unit):
            g, part = divmod(unit, UNITS_PER_GROUP)
            if unit not in units or part < UNITS_PER_GROUP - 1:
                return
            pooled = live.pop(("pooled", g))
            spread = per_unit.tile([P, HALVES, LINES_PER_GROUP, COPIES], F32)
            x2_ps = psum_s.tile([P, G], F32, tag="small")
            for c in range(HALVES):
                nc.vector.tensor_scalar(
                    out=spread[:, c, :, :],
                    in0=pooled[:, c, :].unsqueeze(2).to_broadcast([P, LINES_PER_GROUP, COPIES]),
                    scalar1=b2_col(c),
                    scalar2=None,
                    op0=ALU.add,
                )
                nc.tensor.transpose(
                    x2_ps[:, c * P : (c + 1) * P],
                    spread[:, c, :, :].rearrange("p b d -> p (b d)"),
                    ident[:],
                )
            x2 = per_unit.tile([P, G], F32)
            nc.scalar.copy(out=x2[:], in_=x2_ps[:])
            nc.sync.dma_start(
                out=out_flat[g * GROUP : (g + 1) * GROUP, G : 2 * G].rearrange(
                    "(q i) c -> q i c", i=ROWS_PER_COPY
                ),
                in_=x2[:].unsqueeze(1).to_broadcast([P, ROWS_PER_COPY, G]),
            )

        for k in range(N_UNITS + S_POOL):
            outputs(k - S_OUTPUTS)
            second_matmuls(k - S_SECOND)
            bias_and_squares(k - S_NORM)
            copy_x(k - S_COPY_X)
            normalise(k - S_NORM)
            to_features(k - S_FEATURES)
            regroup_r(k - S_QUANTISE_R)
            first_matmul(k - S_FIRST)
            pool(k - S_POOL)
            quantise_r(k - S_QUANTISE_R)
            transpose_x(k - S_TRANSPOSE_X)
            if k == S_COPY_X:
                spread_constants()
            if k == S_FEATURES:
                w2_q["codes"], w2_q["scales"] = quantise_weight(w2_raw, G, "w2")
